import numpy as np
import ml_dtypes


def mxq(x, axis, fmt="e4m3"):
    dtype, down = {"e4m3": (ml_dtypes.float8_e4m3fn, 7), "e5m2": (ml_dtypes.float8_e5m2, 14)}[fmt]
    v = np.moveaxis(np.asarray(x, np.float32).astype(ml_dtypes.bfloat16).astype(np.float64), axis, -1)
    blocks = v.reshape(v.shape[:-1] + (-1, 32))
    amax = np.abs(blocks).max(-1, keepdims=True)
    byte = np.maximum(np.where(amax > 0, np.frexp(amax)[1] - 1 + 127, 0) - down, 1)
    scale = np.exp2(byte - 127.0)
    codes = (blocks / scale).astype(np.float32).astype(dtype).astype(np.float64)
    return np.moveaxis((codes * scale).reshape(v.shape), -1, axis)


WIDE = False


def mx_kscale(k):
    if not WIDE:
        return np.ones(k)
    levels = np.array([10, -10, 5, -5, 0])
    if k % 512:
        return np.exp2(np.random.permutation(np.resize(levels, k // 32))).repeat(32)
    a = np.empty((k // 512, 16))
    for p in range(k // 512):
        a[p, :8] = np.random.permutation(np.resize(levels, 8))
        for g in range(8):
            far = levels[np.abs(levels - a[p, g]) >= 10]
            a[p, g + 8] = far[np.random.randint(len(far))]
    return np.exp2(a.ravel()).repeat(32)


BF16 = ml_dtypes.bfloat16


def bf(x):
    return np.asarray(x, np.float32).astype(BF16)


def f64(x):
    return np.asarray(x).astype(np.float64)


N, K, H = 1024, 512, 512
G = 4 * H


def sigmoid(v):
    return 1.0 / (1.0 + np.exp(-v))


def used(a):
    return np.concatenate([a[:H], a[2 * H:]], axis=0)


def dgates(z, dh):
    i = sigmoid(z[:, :H])
    g = np.tanh(z[:, 2 * H:3 * H])
    o = sigmoid(z[:, 3 * H:])
    t = np.tanh(i * g)
    dc = dh * o * (1.0 - t * t)
    dzi = dc * g * i * (1.0 - i)
    dzg = dc * i * (1.0 - g * g)
    dzo = dh * t * o * (1.0 - o)
    return np.concatenate([dzi, dzg, dzo], axis=1)


def setup_inputs():
    s = mx_kscale(N)[:, None]
    r = mx_kscale(6 * H)
    u_f, u_b = r[:H], r[3 * H:4 * H]
    V0 = bf(np.random.standard_normal((N, K)))
    wf0 = bf(np.random.standard_normal((G, K)) * 1.5 / np.sqrt(K))
    whf = bf(np.random.standard_normal((G, H)) / np.sqrt(H))
    bif = bf(np.random.standard_normal(G) * 0.3)
    bhf = bf(np.random.standard_normal(G) * 0.3)
    wb0 = bf(np.random.standard_normal((G, K)) * 1.5 / np.sqrt(K))
    whb = bf(np.random.standard_normal((G, H)) / np.sqrt(H))
    bib = bf(np.random.standard_normal(G) * 0.3)
    bhb = bf(np.random.standard_normal(G) * 0.3)
    g = bf(np.random.standard_normal((N, 2 * H)) * np.exp2(np.random.randint(-6, 1, (N, 1))) * 16.0
           / s * np.concatenate([u_f, u_b])[None, :])
    gates_f = f64(V0) @ f64(wf0).T + f64(bif) + f64(bhf)
    gates_b = f64(V0) @ f64(wb0).T + f64(bib) + f64(bhb)
    return {
        "V_cells": bf(f64(V0) * s),
        "w_ih_f": bf(f64(wf0) / np.tile(u_f, 4)[:, None]),
        "w_hh_f": whf,
        "b_ih_f": bif,
        "b_hh_f": bhf,
        "w_ih_b": bf(f64(wb0) / np.tile(u_b, 4)[:, None]),
        "w_hh_b": whb,
        "b_ih_b": bib,
        "b_hh_b": bhb,
        "gates_f": np.asarray(gates_f, np.float32),
        "gates_b": np.asarray(gates_b, np.float32),
        "grad_out": g,
    }


def reference(V_cells, w_ih_f, w_hh_f, b_ih_f, b_hh_f, w_ih_b, w_hh_b, b_ih_b, b_hh_b, gates_f, gates_b, grad_out):
    go = f64(grad_out)
    dz_f = dgates(f64(gates_f), go[:, :H])
    dz_b = dgates(f64(gates_b), go[:, H:])
    dz = np.concatenate([dz_f, dz_b], axis=1)
    w = np.concatenate([used(f64(w_ih_f)), used(f64(w_ih_b))], axis=0)
    dx = mxq(dz, 1, "e5m2") @ mxq(w, 0, "e4m3")
    dwu = mxq(dz_f, 0, "e5m2").T @ mxq(f64(V_cells), 0, "e4m3")
    dw = np.concatenate([dwu[:H], np.zeros((H, K)), dwu[H:]], axis=0)
    return dx, dw

@@ -1,0 +1,358 @@
+from contextlib import ExitStack
+
+import concourse.mybir as mybir
+from concourse.masks import make_identity
+
+N_TOK, K_IN, H = 1024, 512, 512
+FLOPS = 2 * N_TOK * 6 * H * K_IN + 2 * 3 * H * N_TOK * K_IN
+BYTES = (
+    2 * N_TOK * 3 * H * 4
+    + N_TOK * 2 * H * 2
+    + N_TOK * K_IN * 2
+    + 2 * 3 * H * K_IN * 2
+    + N_TOK * K_IN * 4
+    + 4 * H * K_IN * 4
+)
+
+F32 = mybir.dt.float32
+BF16 = mybir.dt.bfloat16
+U32 = mybir.dt.uint32
+U8 = mybir.dt.uint8
+E4 = mybir.dt.float8_e4m3fn_x4
+E5 = mybir.dt.float8_e5m2_x4
+AF = mybir.ActivationFunctionType
+ALU = mybir.AluOpType
+
+P = 128
+GI, GG, GO = 0, 1, 2
+W_ROW0 = (0, 2 * H, 3 * H)
+NSUB = 8
+MANUAL = False
+
+
+def tile_predictionbilstm_t_v_kernel(
+    tc,
+    V_cells,
+    w_ih_f,
+    w_hh_f,
+    b_ih_f,
+    b_hh_f,
+    w_ih_b,
+    w_hh_b,
+    b_ih_b,
+    b_hh_b,
+    gates_f,
+    gates_b,
+    grad_out,
+    out_0,
+    out_1,
+):
+    nc = tc.nc
+    gates = (gates_f, gates_b)
+    w_ih = (w_ih_f, w_ih_b)
+
+    with ExitStack() as ctx:
+        if MANUAL:
+            ctx.enter_context(tc.manual_schedule())
+        const = ctx.enter_context(tc.tile_pool(name="const", bufs=1))
+        zin = ctx.enter_context(tc.tile_pool(name="zin", bufs=4))
+        tmp = ctx.enter_context(tc.tile_pool(name="tmp", bufs=2))
+        dzp = ctx.enter_context(tc.tile_pool(name="dzp", bufs=2))
+        stage = ctx.enter_context(tc.tile_pool(name="stage", bufs=3))
+        keep = ctx.enter_context(tc.tile_pool(name="keep", bufs=1))
+        outp = ctx.enter_context(tc.tile_pool(name="outp", bufs=2))
+        psx = ctx.enter_context(tc.psum_pool(name="psx", bufs=2))
+        ps0 = ctx.enter_context(tc.psum_pool(name="ps0", bufs=4))
+        ps1 = ctx.enter_context(tc.psum_pool(name="ps1", bufs=2))
+
+        warm = const.tile([P, 8], F32, name="warm")
+        nc.vector.memset(warm[:], 0.0)
+        warm2 = const.tile([P, 8], F32, name="warm2")
+        nc.scalar.activation(out=warm2[:], in_=warm[:], func=AF.Tanh)
+        ident = const.tile([P, P], F32, name="ident")
+        make_identity(nc, ident[:])
+        zero = const.tile([P, K_IN], F32, name="zero")
+        nc.gpsimd.memset(zero[:], 0.0)
+
+        w_codes = keep.tile([P, 6, K_IN], U32, name="w_codes", align_bytes=64)
+        w_scales = keep.tile([P, 6, K_IN], U8, name="w_scales", align_bytes=64)
+        v_codes = keep.tile([P, 2, K_IN], U32, name="v_codes", align_bytes=64)
+        v_scales = keep.tile([P, 2, K_IN], U8, name="v_scales", align_bytes=64)
+        tm_codes = keep.tile([P, 2, 3 * H], U32, name="tm_codes", align_bytes=64)
+        tm_scales = keep.tile([P, 2, 3 * H], U8, name="tm_scales", align_bytes=64)
+        ft_codes = keep.tile([P, 6, 8, P], U32, name="ft_codes", align_bytes=64)
+        ft_scales = keep.tile([P, 6, 8, P], U8, name="ft_scales", align_bytes=64)
+
+        zi, zgo, dh = {}, {}, {}
+        c2, tt, t2, g2, pp = {}, {}, {}, {}, {}
+        dzt = {}
+        xts, gts = {}, {}
+        raws, grps = {}, {}
+        acc0 = {}
+
+        def sub(s):
+            return s // 4, (s % 4) // 2, s % 2
+
+        def load(s):
+            d, h, jp = sub(s)
+            rows = slice(512 * h, 512 * (h + 1))
+            js = slice(2 * jp, 2 * jp + 2)
+            gsrc = gates[d][rows, :].rearrange("(p j) c -> p j c", j=4)
+            zi_t = zin.tile([P, 2, H], F32, name="zi")
+            nc.sync.dma_start(out=zi_t[:], in_=gsrc[:, js, 0:H])
+            zgo_t = zin.tile([P, 2, 2 * H], F32, name="zgo")
+            nc.sync.dma_start(out=zgo_t[:], in_=gsrc[:, js, 2 * H : 4 * H])
+            dh_t = zin.tile([P, 2, H], BF16, name="dh")
+            dsrc = grad_out[rows, H * d : H * (d + 1)].rearrange("(p j) c -> p j c", j=4)
+            nc.sync.dma_start(out=dh_t[:], in_=dsrc[:, js, :])
+            zi[s], zgo[s], dh[s] = zi_t, zgo_t, dh_t
+
+        def a_of(s):
+            return zi[s][:]
+
+        def g_of(s):
+            return zgo[s][:, :, 0:H]
+
+        def b_of(s):
+            return zgo[s][:, :, H : 2 * H]
+
+        def act_a(s):
+            nc.scalar.activation(out=a_of(s), in_=a_of(s), func=AF.Tanh, scale=0.5)
+            nc.scalar.activation(out=g_of(s), in_=g_of(s), func=AF.Tanh)
+            nc.scalar.activation(out=b_of(s), in_=b_of(s), func=AF.Tanh, scale=0.5)
+
+        def stt(out, in0, scalar, in1, op0):
+            nc.vector.scalar_tensor_tensor(out=out, in0=in0, scalar=scalar, in1=in1, op0=op0, op1=ALU.mult)
+
+        def v_c2(s):
+            c2_t = tmp.tile([P, 2, H], F32, name="c2")
+            c2[s] = c2_t
+            stt(c2_t[:], a_of(s), 1.0, g_of(s), ALU.add)
+
+        def act_c(s):
+            t_t = tmp.tile([P, 2, H], F32, name="tt")
+            tt[s] = t_t
+            nc.scalar.activation(out=t_t[:], in_=c2[s][:], func=AF.Tanh, scale=0.5)
+            t2_t = tmp.tile([P, 2, H], F32, name="t2")
+            t2[s] = t2_t
+            nc.scalar.activation(out=t2_t[:], in_=t_t[:], func=AF.Square)
+            g2_t = tmp.tile([P, 2, H], F32, name="g2")
+            g2[s] = g2_t
+            nc.scalar.activation(out=g2_t[:], in_=g_of(s), func=AF.Square, scale=0.5)
+
+        def dz_out(s, x):
+            d, h, jp = sub(s)
+            return dzt[(d, h)][:, x, 2 * jp : 2 * jp + 2, :]
+
+        def v_first(s):
+            d, h, jp = sub(s)
+            if jp == 0:
+                dz_t = dzp.tile([P, 3, 4, H], BF16, name="dz")
+                dzt[(d, h)] = dz_t
+            p_t = tmp.tile([P, 2, H], F32, name="pp", bufs=1)
+            pp[s] = p_t
+            stt(p_t[:], b_of(s), 1.0, dh[s][:], ALU.add)
+            stt(tt[s][:], b_of(s), 1.0, tt[s][:], ALU.subtract)
+            stt(t2[s][:], t2[s][:], 1.0, p_t[:], ALU.subtract)
+            stt(dz_out(s, GO), tt[s][:], -0.25, p_t[:], ALU.mult)
+
+        def v_second(s):
+            stt(c2[s][:], a_of(s), 1.0, c2[s][:], ALU.subtract)
+            stt(pp[s][:], a_of(s), 1.0, t2[s][:], ALU.add)
+            stt(dz_out(s, GI), t2[s][:], 0.125, c2[s][:], ALU.mult)
+
+        def v_third(s):
+            stt(dz_out(s, GG), g2[s][:], 0.25, pp[s][:], ALU.subtract)
+
+        def transposes(s, x):
+            d, h, jp = sub(s)
+            xt = psx.tile([P, 2, 2, P], F32, name="xt")
+            xts[(s, x)] = xt
+            for jj in range(2):
+                words = dzt[(d, h)][:, x, 2 * jp + jj, :].bitcast(F32)
+                for u in range(2):
+                    nc.tensor.transpose(xt[:, jj, u, :], words[:, u : H // 2 : 2], ident[:])
+
+        def evac_t(s, x):
+            gt = stage.tile([P, 2, P, 4], BF16, name="gt", align_bytes=64)
+            gts[(s, x)] = gt
+            nc.scalar.copy(out=gt[:].bitcast(F32), in_=xts[(s, x)][:].rearrange("q a u p -> q a p u"))
+
+        def quant_t(s, x):
+            d, h, jp = sub(s)
+            a0 = 4 * h + 2 * jp
+            g = 3 * d + x
+            nc.vector.quantize_mx(
+                out=ft_codes[:, g, a0 : a0 + 2, :].rearrange("q a p -> q (a p)").bitcast(E5),
+                scales=ft_scales[:, g, a0 : a0 + 2, :].rearrange("q a p -> q (a p)"),
+                in_=gts[(s, x)][:].rearrange("q a p t -> q (a p t)"),
+            )
+
+        def mm0(s, g, start, stop):
+            d, h, jp = sub(s)
+            for jj in range(2):
+                a = 4 * h + 2 * jp + jj
+                nc.tensor.matmul_mx(
+                    out=acc0[(s, jj)][:],
+                    lhsT=ft_codes[:, g, a, :].bitcast(E5),
+                    lhsT_scale=ft_scales[:, g, a, :],
+                    rhs=w_codes[:, g, :].bitcast(E4),
+                    rhs_scale=w_scales[:, g, :],
+                    start=start,
+                    stop=stop,
+                )
+
+        def mm0_open(s):
+            for jj in range(2):
+                acc = ps0.tile([P, K_IN], F32, name="acc0")
+                acc0[(s, jj)] = acc
+            for g in range(3):
+                mm0(s, g, g == 0, False)
+
+        def finish0(s):
+            d, h, jp = sub(s)
+            o0 = outp.tile([P, 2, K_IN], F32, name="o0")
+            nc.scalar.copy(out=o0[:, 0, :], in_=acc0[(s, 0)][:])
+            nc.vector.tensor_copy(out=o0[:, 1, :], in_=acc0[(s, 1)][:])
+            dst = out_0[512 * h : 512 * (h + 1), :].rearrange("(p j) c -> p j c", j=4)
+            nc.sync.dma_start(out=dst[:, 2 * jp : 2 * jp + 2, :], in_=o0[:])
+
+        def load_rows(key, src):
+            raw = stage.tile([P, 4, K_IN], BF16, name="raw")
+            raws[key] = raw
+            nc.sync.dma_start(out=raw[:], in_=src.rearrange("(p j) c -> p j c", j=4))
+
+        def load_w(g):
+            d, x = g // 3, g % 3
+            load_rows(("w", g), w_ih[d][W_ROW0[x] : W_ROW0[x] + H, :])
+
+        def load_v(h):
+            load_rows(("v", h), V_cells[512 * h : 512 * (h + 1), :])
+
+        def interleave(key, src, on_vector):
+            grp = stage.tile([P, K_IN, 4], BF16, name="grp", align_bytes=64)
+            grps[key] = grp
+            if on_vector:
+                nc.vector.tensor_copy(out=grp[:], in_=src.rearrange("p j c -> p c j"))
+            else:
+                nc.scalar.copy(out=grp[:], in_=src.rearrange("p j c -> p c j"))
+
+        def quant_rows(key, codes, scales, fmt):
+            nc.vector.quantize_mx(
+                out=codes.bitcast(fmt),
+                scales=scales,
+                in_=grps[key][:].rearrange("p c j -> p (c j)"),
+            )
+
+        def prep_w(g, on_vector):
+            interleave(("w", g), raws[("w", g)][:], on_vector)
+            quant_rows(("w", g), w_codes[:, g, :], w_scales[:, g, :], E4)
+
+        def prep_v(h, on_vector):
+            interleave(("v", h), raws[("v", h)][:], on_vector)
+            quant_rows(("v", h), v_codes[:, h, :], v_scales[:, h, :], E4)
+
+        def prep_tm(h, x, on_vector):
+            interleave(("t", h, x), dzt[(0, h)][:, x, :, :], on_vector)
+            cols = slice(H * x, H * (x + 1))
+            quant_rows(("t", h, x), tm_codes[:, h, cols], tm_scales[:, h, cols], E5)
+
+        def out1(x):
+            for m in range(4):
+                cols = slice(H * x + P * m, H * x + P * (m + 1))
+                acc = ps1.tile([P, K_IN], F32, name="acc1")
+                for h in range(2):
+                    nc.tensor.matmul_mx(
+                        out=acc[:],
+                        lhsT=tm_codes[:, h, cols].bitcast(E5),
+                        lhsT_scale=tm_scales[:, h, cols],
+                        rhs=v_codes[:, h, :].bitcast(E4),
+                        rhs_scale=v_scales[:, h, :],
+                        start=(h == 0),
+                        stop=(h == 1),
+                    )
+                o1 = outp.tile([P, K_IN], F32, name="o1", bufs=3)
+                nc.scalar.copy(out=o1[:], in_=acc[:])
+                r0 = W_ROW0[x] + P * m
+                nc.sync.dma_start(out=out_1[r0 : r0 + P, :], in_=o1[:])
+
+        def late(s):
+            d, h, jp = sub(s)
+            quant_t(s, GI)
+            if d == 1:
+                mm0(s, 3 + GI, False, False)
+            quant_t(s, GG)
+            if d == 1:
+                mm0(s, 3 + GG, False, True)
+                finish0(s)
+
+        def extras(s):
+            if s == 0:
+                prep_w(0, True)
+                prep_w(3, False)
+                prep_v(0, False)
+                load_w(1)
+                load_w(4)
+                load_v(1)
+            if s == 1:
+                prep_w(1, True)
+                prep_w(4, False)
+                prep_v(1, False)
+                load_w(2)
+                load_w(5)
+            if s == 2:
+                prep_w(2, True)
+                prep_w(5, False)
+                prep_tm(0, GO, False)
+                for r in range(4):
+                    nc.sync.dma_start(out=out_1[H + P * r : H + P * (r + 1), :], in_=zero[:])
+            if s == 3:
+                prep_tm(0, GI, False)
+                prep_tm(0, GG, False)
+            if s == 4:
+                prep_tm(1, GO, True)
+                prep_tm(1, GI, True)
+                prep_tm(1, GG, False)
+                out1(GO)
+            if s == 5:
+                out1(GI)
+            if s == 6:
+                out1(GG)
+
+        load(0)
+        load(1)
+        load_w(0)
+        load_w(3)
+        load_v(0)
+        load(2)
+        load(3)
+        act_a(0)
+        v_c2(0)
+        act_c(0)
+        act_a(1)
+        for s in range(NSUB):
+            if s + 1 < NSUB:
+                v_c2(s + 1)
+                act_c(s + 1)
+            if s >= 1:
+                late(s - 1)
+            if s >= 4:
+                mm0_open(s)
+            v_first(s)
+            transposes(s, GO)
+            if s + 2 < NSUB:
+                act_a(s + 2)
+            evac_t(s, GO)
+            v_second(s)
+            transposes(s, GI)
+            evac_t(s, GI)
+            quant_t(s, GO)
+            if s >= 4:
+                mm0(s, 3 + GO, False, False)
+            v_third(s)
+            transposes(s, GG)
+            evac_t(s, GG)
+            extras(s)
+            if s + 4 < NSUB:
+                load(s + 4)
+        late(NSUB - 1)

@@ -27,7 +27,6 @@ P = 128
 GI, GG, GO = 0, 1, 2
 W_ROW0 = (0, 2 * H, 3 * H)
 NSUB = 8
-MANUAL = False
 
 
 def tile_predictionbilstm_t_v_kernel(
@@ -52,25 +51,24 @@ def tile_predictionbilstm_t_v_kernel(
     w_ih = (w_ih_f, w_ih_b)
 
     with ExitStack() as ctx:
-        if MANUAL:
-            ctx.enter_context(tc.manual_schedule())
         const = ctx.enter_context(tc.tile_pool(name="const", bufs=1))
-        zin = ctx.enter_context(tc.tile_pool(name="zin", bufs=4))
-        tmp = ctx.enter_context(tc.tile_pool(name="tmp", bufs=2))
-        dzp = ctx.enter_context(tc.tile_pool(name="dzp", bufs=2))
-        stage = ctx.enter_context(tc.tile_pool(name="stage", bufs=3))
+        zin = ctx.enter_context(tc.tile_pool(name="zin", bufs=3))
+        fm = ctx.enter_context(tc.tile_pool(name="fm", bufs=3))
+        gp = ctx.enter_context(tc.tile_pool(name="gp", bufs=4))
+        stage = ctx.enter_context(tc.tile_pool(name="stage", bufs=2))
         keep = ctx.enter_context(tc.tile_pool(name="keep", bufs=1))
         outp = ctx.enter_context(tc.tile_pool(name="outp", bufs=2))
-        psx = ctx.enter_context(tc.psum_pool(name="psx", bufs=2))
-        ps0 = ctx.enter_context(tc.psum_pool(name="ps0", bufs=4))
-        ps1 = ctx.enter_context(tc.psum_pool(name="ps1", bufs=2))
+        pst = ctx.enter_context(tc.psum_pool(name="pst", bufs=6))
+        psm = ctx.enter_context(tc.psum_pool(name="psm", bufs=2))
 
         warm = const.tile([P, 8], F32, name="warm")
         nc.vector.memset(warm[:], 0.0)
         warm2 = const.tile([P, 8], F32, name="warm2")
-        nc.scalar.activation(out=warm2[:], in_=warm[:], func=AF.Tanh)
+        nc.scalar.activation(out=warm2[:], in_=warm[:], func=AF.Sigmoid)
         ident = const.tile([P, P], F32, name="ident")
         make_identity(nc, ident[:])
+        ident_bf = const.tile([P, P], BF16, name="ident_bf")
+        make_identity(nc, ident_bf[:])
         zero = const.tile([P, K_IN], F32, name="zero")
         nc.gpsimd.memset(zero[:], 0.0)
 
@@ -80,15 +78,15 @@ def tile_predictionbilstm_t_v_kernel(
         v_scales = keep.tile([P, 2, K_IN], U8, name="v_scales", align_bytes=64)
         tm_codes = keep.tile([P, 2, 3 * H], U32, name="tm_codes", align_bytes=64)
         tm_scales = keep.tile([P, 2, 3 * H], U8, name="tm_scales", align_bytes=64)
-        ft_codes = keep.tile([P, 6, 8, P], U32, name="ft_codes", align_bytes=64)
-        ft_scales = keep.tile([P, 6, 8, P], U8, name="ft_scales", align_bytes=64)
+        ff_codes = keep.tile([P, 3, 8, P], U32, name="ff_codes", align_bytes=64)
+        ff_scales = keep.tile([P, 3, 8, P], U8, name="ff_scales", align_bytes=64)
 
-        zi, zgo, dh = {}, {}, {}
-        c2, tt, t2, g2, pp = {}, {}, {}, {}, {}
-        dzt = {}
-        xts, gts = {}, {}
+        zi, zgo, dh, pt = {}, {}, {}, {}
+        gg, g2, cc, tt, t2 = {}, {}, {}, {}, {}
+        bank = {}
+        gz = {}
+        fb_codes, fb_scales = {}, {}
         raws, grps = {}, {}
-        acc0 = {}
 
         def sub(s):
             return s // 4, (s % 4) // 2, s % 2
@@ -99,126 +97,135 @@ def tile_predictionbilstm_t_v_kernel(
             js = slice(2 * jp, 2 * jp + 2)
             gsrc = gates[d][rows, :].rearrange("(p j) c -> p j c", j=4)
             zi_t = zin.tile([P, 2, H], F32, name="zi")
-            nc.sync.dma_start(out=zi_t[:], in_=gsrc[:, js, 0:H])
             zgo_t = zin.tile([P, 2, 2 * H], F32, name="zgo")
-            nc.sync.dma_start(out=zgo_t[:], in_=gsrc[:, js, 2 * H : 4 * H])
+            if s == 0:
+                for jj in range(2):
+                    nc.sync.dma_start(out=zgo_t[:, jj, 0:H], in_=gsrc[:, jj, 2 * H : 3 * H])
+                    nc.sync.dma_start(out=zi_t[:, jj, :], in_=gsrc[:, jj, 0:H])
+                nc.sync.dma_start(out=zgo_t[:, :, H : 2 * H], in_=gsrc[:, js, 3 * H : 4 * H])
+            else:
+                nc.sync.dma_start(out=zi_t[:], in_=gsrc[:, js, 0:H])
+                nc.sync.dma_start(out=zgo_t[:], in_=gsrc[:, js, 2 * H : 4 * H])
             dh_t = zin.tile([P, 2, H], BF16, name="dh")
             dsrc = grad_out[rows, H * d : H * (d + 1)].rearrange("(p j) c -> p j c", j=4)
             nc.sync.dma_start(out=dh_t[:], in_=dsrc[:, js, :])
             zi[s], zgo[s], dh[s] = zi_t, zgo_t, dh_t
 
-        def a_of(s):
-            return zi[s][:]
-
-        def g_of(s):
-            return zgo[s][:, :, 0:H]
-
-        def b_of(s):
-            return zgo[s][:, :, H : 2 * H]
-
-        def act_a(s):
-            nc.scalar.activation(out=a_of(s), in_=a_of(s), func=AF.Tanh, scale=0.5)
-            nc.scalar.activation(out=g_of(s), in_=g_of(s), func=AF.Tanh)
-            nc.scalar.activation(out=b_of(s), in_=b_of(s), func=AF.Tanh, scale=0.5)
-
         def stt(out, in0, scalar, in1, op0):
             nc.vector.scalar_tensor_tensor(out=out, in0=in0, scalar=scalar, in1=in1, op0=op0, op1=ALU.mult)
 
-        def v_c2(s):
-            c2_t = tmp.tile([P, 2, H], F32, name="c2")
-            c2[s] = c2_t
-            stt(c2_t[:], a_of(s), 1.0, g_of(s), ALU.add)
+        def act_io(s):
+            if s == 0:
+                for jj in range(2):
+                    nc.scalar.activation(out=zi[s][:, jj, :], in_=zi[s][:, jj, :], func=AF.Sigmoid)
+            else:
+                nc.scalar.activation(out=zi[s][:], in_=zi[s][:], func=AF.Sigmoid)
+            o_ap = zgo[s][:, :, H : 2 * H]
+            nc.scalar.activation(out=o_ap, in_=o_ap, func=AF.Sigmoid)
 
-        def act_c(s):
-            t_t = tmp.tile([P, 2, H], F32, name="tt")
-            tt[s] = t_t
-            nc.scalar.activation(out=t_t[:], in_=c2[s][:], func=AF.Tanh, scale=0.5)
-            t2_t = tmp.tile([P, 2, H], F32, name="t2")
-            t2[s] = t2_t
-            nc.scalar.activation(out=t2_t[:], in_=t_t[:], func=AF.Square)
-            g2_t = tmp.tile([P, 2, H], F32, name="g2")
-            g2[s] = g2_t
-            nc.scalar.activation(out=g2_t[:], in_=g_of(s), func=AF.Square, scale=0.5)
+        def gp_p(s):
+            p_t = zin.tile([P, 2, H], F32, name="pt", bufs=2)
+            pt[s] = p_t
+            nc.gpsimd.tensor_tensor(out=p_t[:], in0=zgo[s][:, :, H : 2 * H], in1=dh[s][:], op=ALU.mult)
 
-        def dz_out(s, x):
-            d, h, jp = sub(s)
-            return dzt[(d, h)][:, x, 2 * jp : 2 * jp + 2, :]
+        def turn(key, src, c0):
+            b_t = pst.tile([P, 4, P], F32, name="bk")
+            bank[key] = b_t
+            for t in range(4):
+                nc.tensor.transpose(b_t[:, t, :], src[:, c0 + t : c0 + H : 4], ident[:])
 
-        def v_first(s):
-            d, h, jp = sub(s)
-            if jp == 0:
-                dz_t = dzp.tile([P, 3, 4, H], BF16, name="dz")
-                dzt[(d, h)] = dz_t
-            p_t = tmp.tile([P, 2, H], F32, name="pp", bufs=1)
-            pp[s] = p_t
-            stt(p_t[:], b_of(s), 1.0, dh[s][:], ALU.add)
-            stt(tt[s][:], b_of(s), 1.0, tt[s][:], ALU.subtract)
-            stt(t2[s][:], t2[s][:], 1.0, p_t[:], ALU.subtract)
-            stt(dz_out(s, GO), tt[s][:], -0.25, p_t[:], ALU.mult)
+        def view(key):
+            return bank[key][:].rearrange("q t n -> q n t")
 
-        def v_second(s):
-            stt(c2[s][:], a_of(s), 1.0, c2[s][:], ALU.subtract)
-            stt(pp[s][:], a_of(s), 1.0, t2[s][:], ALU.add)
-            stt(dz_out(s, GI), t2[s][:], 0.125, c2[s][:], ALU.mult)
+        def new_fm(store, s, name, bufs):
+            x_t = fm.tile([P, 2, P, 4], F32, name=name, bufs=bufs)
+            store[s] = x_t
 
-        def v_third(s):
-            stt(dz_out(s, GG), g2[s][:], 0.25, pp[s][:], ALU.subtract)
-
-        def transposes(s, x):
-            d, h, jp = sub(s)
-            xt = psx.tile([P, 2, 2, P], F32, name="xt")
-            xts[(s, x)] = xt
+        def stage_b1(s):
+            new_fm(gg, s, "gg", 2)
+            new_fm(cc, s, "cc", 3)
             for jj in range(2):
-                words = dzt[(d, h)][:, x, 2 * jp + jj, :].bitcast(F32)
-                for u in range(2):
-                    nc.tensor.transpose(xt[:, jj, u, :], words[:, u : H // 2 : 2], ident[:])
+                turn(("z", s, jj), zgo[s][:, jj, :], 0)
+                nc.scalar.activation(out=gg[s][:, jj], in_=view(("z", s, jj)), func=AF.Tanh)
+                turn(("i", s, jj), zi[s][:, jj, :], 0)
+                nc.vector.tensor_tensor(out=cc[s][:, jj], in0=view(("i", s, jj)), in1=gg[s][:, jj], op=ALU.mult)
+            new_fm(g2, s, "g2", 3)
+            nc.scalar.activation(out=g2[s][:], in_=gg[s][:], func=AF.Square)
+            new_fm(tt, s, "tt", 2)
+            nc.scalar.activation(out=tt[s][:], in_=cc[s][:], func=AF.Tanh, scale=-1.0)
+            new_fm(t2, s, "t2", 3)
+            nc.scalar.activation(out=t2[s][:], in_=tt[s][:], func=AF.Square)
 
-        def evac_t(s, x):
-            gt = stage.tile([P, 2, P, 4], BF16, name="gt", align_bytes=64)
-            gts[(s, x)] = gt
-            nc.scalar.copy(out=gt[:].bitcast(F32), in_=xts[(s, x)][:].rearrange("q a u p -> q a p u"))
+        def stage_b2(s):
+            for jj in range(2):
+                stt(g2[s][:, jj], g2[s][:, jj], 1.0, view(("i", s, jj)), ALU.subtract)
+            for jj in range(2):
+                stt(cc[s][:, jj], view(("i", s, jj)), 1.0, cc[s][:, jj], ALU.subtract)
+
+        def stage_c(s, tail_on_vector):
+            gz_t = gp.tile([P, 3, 2, P, 4], BF16, name="gz", align_bytes=64)
+            gz[s] = gz_t
+            for jj in range(2):
+                turn(("o", s, jj), zgo[s][:, jj, :], H)
+                turn(("p", s, jj), pt[s][:, jj, :], 0)
+                stt(tt[s][:, jj], view(("o", s, jj)), 1.0, tt[s][:, jj], ALU.subtract)
+                stt(t2[s][:, jj], t2[s][:, jj], 1.0, view(("p", s, jj)), ALU.subtract)
+                nc.vector.tensor_tensor(out=gz_t[:, GO, jj], in0=view(("p", s, jj)), in1=tt[s][:, jj], op=ALU.mult)
+            eng = nc.vector if tail_on_vector else nc.gpsimd
+            eng.tensor_tensor(out=gz_t[:, GI], in0=t2[s][:], in1=cc[s][:], op=ALU.mult)
+            eng.tensor_tensor(out=gz_t[:, GG], in0=t2[s][:], in1=g2[s][:], op=ALU.mult)
+
+        def ft_slices(s, x):
+            d, h, jp = sub(s)
+            if d == 0:
+                a0 = 4 * h + 2 * jp
+                return ff_codes[:, x, a0 : a0 + 2, :], ff_scales[:, x, a0 : a0 + 2, :]
+            return fb_codes[s][:, x], fb_scales[s][:, x]
 
         def quant_t(s, x):
             d, h, jp = sub(s)
-            a0 = 4 * h + 2 * jp
-            g = 3 * d + x
+            if d == 1 and s not in fb_codes:
+                c_t = gp.tile([P, 3, 2, P], U32, name="fbc", bufs=2, align_bytes=64)
+                s_t = gp.tile([P, 3, 2, P], U8, name="fbs", bufs=2, align_bytes=64)
+                fb_codes[s], fb_scales[s] = c_t, s_t
+            codes, scales = ft_slices(s, x)
             nc.vector.quantize_mx(
-                out=ft_codes[:, g, a0 : a0 + 2, :].rearrange("q a p -> q (a p)").bitcast(E5),
-                scales=ft_scales[:, g, a0 : a0 + 2, :].rearrange("q a p -> q (a p)"),
-                in_=gts[(s, x)][:].rearrange("q a p t -> q (a p t)"),
+                out=codes.rearrange("q a p -> q (a p)").bitcast(E5),
+                scales=scales.rearrange("q a p -> q (a p)"),
+                in_=gz[s][:, x].rearrange("q a p t -> q (a p t)"),
             )
 
-        def mm0(s, g, start, stop):
-            d, h, jp = sub(s)
-            for jj in range(2):
-                a = 4 * h + 2 * jp + jj
+        def unit0(s, jj, o0):
+            acc = psm.tile([P, K_IN], F32, name="pm")
+            for g in range(6):
+                codes, scales = ft_slices(s - 4 * (1 - g // 3), g % 3)
                 nc.tensor.matmul_mx(
-                    out=acc0[(s, jj)][:],
-                    lhsT=ft_codes[:, g, a, :].bitcast(E5),
-                    lhsT_scale=ft_scales[:, g, a, :],
+                    out=acc[:],
+                    lhsT=codes[:, jj, :].bitcast(E5),
+                    lhsT_scale=scales[:, jj, :],
                     rhs=w_codes[:, g, :].bitcast(E4),
                     rhs_scale=w_scales[:, g, :],
-                    start=start,
-                    stop=stop,
+                    start=(g == 0),
+                    stop=(g == 5),
                 )
+            if jj == 0:
+                nc.scalar.copy(out=o0[:, jj, :], in_=acc[:])
+            else:
+                nc.vector.tensor_copy(out=o0[:, jj, :], in_=acc[:])
 
-        def mm0_open(s):
-            for jj in range(2):
-                acc = ps0.tile([P, K_IN], F32, name="acc0")
-                acc0[(s, jj)] = acc
-            for g in range(3):
-                mm0(s, g, g == 0, False)
-
-        def finish0(s):
+        def stage_q(s):
             d, h, jp = sub(s)
-            o0 = outp.tile([P, 2, K_IN], F32, name="o0")
-            nc.scalar.copy(out=o0[:, 0, :], in_=acc0[(s, 0)][:])
-            nc.vector.tensor_copy(out=o0[:, 1, :], in_=acc0[(s, 1)][:])
-            dst = out_0[512 * h : 512 * (h + 1), :].rearrange("(p j) c -> p j c", j=4)
-            nc.sync.dma_start(out=dst[:, 2 * jp : 2 * jp + 2, :], in_=o0[:])
+            for x in (GO, GI, GG):
+                quant_t(s, x)
+            if d == 1:
+                o0 = outp.tile([P, 2, K_IN], F32, name="o0")
+                for jj in range(2):
+                    unit0(s, jj, o0)
+                dst = out_0[512 * h : 512 * (h + 1), :].rearrange("(p j) c -> p j c", j=4)
+                nc.sync.dma_start(out=dst[:, 2 * jp : 2 * jp + 2, :], in_=o0[:])
 
         def load_rows(key, src):
-            raw = stage.tile([P, 4, K_IN], BF16, name="raw")
+            raw = stage.tile([P, 4, K_IN], BF16, name="raw", bufs=3)
             raws[key] = raw
             nc.sync.dma_start(out=raw[:], in_=src.rearrange("(p j) c -> p j c", j=4))
 
@@ -229,38 +236,46 @@ def tile_predictionbilstm_t_v_kernel(
         def load_v(h):
             load_rows(("v", h), V_cells[512 * h : 512 * (h + 1), :])
 
-        def interleave(key, src, on_vector):
+        def prep_rows(key, codes, scales, on_vector):
             grp = stage.tile([P, K_IN, 4], BF16, name="grp", align_bytes=64)
-            grps[key] = grp
+            src = raws[key][:].rearrange("p j c -> p c j")
             if on_vector:
-                nc.vector.tensor_copy(out=grp[:], in_=src.rearrange("p j c -> p c j"))
+                nc.vector.tensor_copy(out=grp[:], in_=src)
             else:
-                nc.scalar.copy(out=grp[:], in_=src.rearrange("p j c -> p c j"))
-
-        def quant_rows(key, codes, scales, fmt):
-            nc.vector.quantize_mx(
-                out=codes.bitcast(fmt),
-                scales=scales,
-                in_=grps[key][:].rearrange("p c j -> p (c j)"),
-            )
+                nc.scalar.copy(out=grp[:], in_=src)
+            nc.vector.quantize_mx(out=codes.bitcast(E4), scales=scales, in_=grp[:].rearrange("p c j -> p (c j)"))
 
         def prep_w(g, on_vector):
-            interleave(("w", g), raws[("w", g)][:], on_vector)
-            quant_rows(("w", g), w_codes[:, g, :], w_scales[:, g, :], E4)
+            prep_rows(("w", g), w_codes[:, g, :], w_scales[:, g, :], on_vector)
 
         def prep_v(h, on_vector):
-            interleave(("v", h), raws[("v", h)][:], on_vector)
-            quant_rows(("v", h), v_codes[:, h, :], v_scales[:, h, :], E4)
+            prep_rows(("v", h), v_codes[:, h, :], v_scales[:, h, :], on_vector)
 
         def prep_tm(h, x, on_vector):
-            interleave(("t", h, x), dzt[(0, h)][:, x, :, :], on_vector)
+            tmg = stage.tile([P, 4, P, 4], BF16, name="tmg", align_bytes=64)
+            for tp in range(2):
+                xt = psm.tile([P, 2, 4, P], BF16, name="pm")
+                for t in range(2):
+                    for j in range(4):
+                        src = gz[2 * h + j // 2][:, x, j % 2, :, 2 * tp + t]
+                        nc.tensor.transpose(xt[:, t, j, :], src, ident_bf[:])
+                dst = tmg[:, 2 * tp : 2 * tp + 2]
+                if on_vector[tp]:
+                    nc.vector.tensor_copy(out=dst, in_=xt[:].rearrange("p t j q -> p t q j"))
+                else:
+                    nc.scalar.copy(out=dst, in_=xt[:].rearrange("p t j q -> p t q j"))
             cols = slice(H * x, H * (x + 1))
-            quant_rows(("t", h, x), tm_codes[:, h, cols], tm_scales[:, h, cols], E5)
+            nc.vector.quantize_mx(
+                out=tm_codes[:, h, cols].bitcast(E5),
+                scales=tm_scales[:, h, cols],
+                in_=tmg[:].rearrange("p t q j -> p (t q j)"),
+            )
 
         def out1(x):
-            for m in range(4):
-                cols = slice(H * x + P * m, H * x + P * (m + 1))
-                acc = ps1.tile([P, K_IN], F32, name="acc1")
+            rows = out_1[W_ROW0[x] : W_ROW0[x] + H, :].rearrange("(q t) c -> q t c", t=4)
+            for t in range(4):
+                cols = slice(H * x + P * t, H * x + P * (t + 1))
+                acc = psm.tile([P, K_IN], F32, name="pm")
                 for h in range(2):
                     nc.tensor.matmul_mx(
                         out=acc[:],
@@ -273,86 +288,63 @@ def tile_predictionbilstm_t_v_kernel(
                     )
                 o1 = outp.tile([P, K_IN], F32, name="o1", bufs=3)
                 nc.scalar.copy(out=o1[:], in_=acc[:])
-                r0 = W_ROW0[x] + P * m
-                nc.sync.dma_start(out=out_1[r0 : r0 + P, :], in_=o1[:])
+                nc.sync.dma_start(out=rows[:, t, :], in_=o1[:])
 
-        def late(s):
-            d, h, jp = sub(s)
-            quant_t(s, GI)
-            if d == 1:
-                mm0(s, 3 + GI, False, False)
-            quant_t(s, GG)
-            if d == 1:
-                mm0(s, 3 + GG, False, True)
-                finish0(s)
-
-        def extras(s):
-            if s == 0:
+        def extras(k):
+            if k == 0:
                 prep_w(0, True)
-                prep_w(3, False)
-                prep_v(0, False)
-                load_w(1)
-                load_w(4)
-                load_v(1)
-            if s == 1:
                 prep_w(1, True)
-                prep_w(4, False)
-                prep_v(1, False)
+                prep_v(0, False)
                 load_w(2)
-                load_w(5)
-            if s == 2:
+                load_w(3)
+                load_v(1)
+            if k == 1:
                 prep_w(2, True)
-                prep_w(5, False)
-                prep_tm(0, GO, False)
+                prep_w(3, True)
+                prep_v(1, False)
+                load_w(4)
+                load_w(5)
+            if k == 2:
+                prep_w(4, True)
+                prep_w(5, True)
                 for r in range(4):
                     nc.sync.dma_start(out=out_1[H + P * r : H + P * (r + 1), :], in_=zero[:])
-            if s == 3:
-                prep_tm(0, GI, False)
-                prep_tm(0, GG, False)
-            if s == 4:
-                prep_tm(1, GO, True)
-                prep_tm(1, GI, True)
-                prep_tm(1, GG, False)
+                prep_tm(0, GO, (False, False))
+                prep_tm(0, GI, (False, True))
+                prep_tm(0, GG, (False, False))
+            if k == 4:
+                prep_tm(1, GO, (False, False))
+                prep_tm(1, GI, (False, True))
+                prep_tm(1, GG, (False, False))
+            if k == 5:
                 out1(GO)
-            if s == 5:
                 out1(GI)
-            if s == 6:
+            if k == 6:
                 out1(GG)
 
-        load(0)
-        load(1)
         load_w(0)
-        load_w(3)
+        load(0)
+        load_w(1)
+        load(1)
         load_v(0)
         load(2)
-        load(3)
-        act_a(0)
-        v_c2(0)
-        act_c(0)
-        act_a(1)
-        for s in range(NSUB):
-            if s + 1 < NSUB:
-                v_c2(s + 1)
-                act_c(s + 1)
-            if s >= 1:
-                late(s - 1)
-            if s >= 4:
-                mm0_open(s)
-            v_first(s)
-            transposes(s, GO)
-            if s + 2 < NSUB:
-                act_a(s + 2)
-            evac_t(s, GO)
-            v_second(s)
-            transposes(s, GI)
-            evac_t(s, GI)
-            quant_t(s, GO)
-            if s >= 4:
-                mm0(s, 3 + GO, False, False)
-            v_third(s)
-            transposes(s, GG)
-            evac_t(s, GG)
-            extras(s)
-            if s + 4 < NSUB:
-                load(s + 4)
-        late(NSUB - 1)
+        act_io(0)
+        gp_p(0)
+        stage_b1(0)
+        stage_b2(0)
+        act_io(1)
+        gp_p(1)
+        for k in range(NSUB):
+            if k + 1 < NSUB:
+                stage_b1(k + 1)
+                stage_b2(k + 1)
+            stage_c(k, k == NSUB - 1)
+            if k + 3 < NSUB:
+                load(k + 3)
+            if k + 2 < NSUB:
+                act_io(k + 2)
+                gp_p(k + 2)
+            if k >= 1:
+                stage_q(k - 1)
+            extras(k)
+        stage_q(NSUB - 1)

@@ -27,6 +27,7 @@ P = 128
 GI, GG, GO = 0, 1, 2
 W_ROW0 = (0, 2 * H, 3 * H)
 NSUB = 8
+MANUAL = False
 
 
 def tile_predictionbilstm_t_v_kernel(
@@ -51,24 +52,25 @@ def tile_predictionbilstm_t_v_kernel(
     w_ih = (w_ih_f, w_ih_b)
 
     with ExitStack() as ctx:
+        if MANUAL:
+            ctx.enter_context(tc.manual_schedule())
         const = ctx.enter_context(tc.tile_pool(name="const", bufs=1))
-        zin = ctx.enter_context(tc.tile_pool(name="zin", bufs=3))
-        fm = ctx.enter_context(tc.tile_pool(name="fm", bufs=3))
-        gp = ctx.enter_context(tc.tile_pool(name="gp", bufs=4))
-        stage = ctx.enter_context(tc.tile_pool(name="stage", bufs=2))
+        zin = ctx.enter_context(tc.tile_pool(name="zin", bufs=4))
+        tmp = ctx.enter_context(tc.tile_pool(name="tmp", bufs=2))
+        dzp = ctx.enter_context(tc.tile_pool(name="dzp", bufs=2))
+        stage = ctx.enter_context(tc.tile_pool(name="stage", bufs=3))
         keep = ctx.enter_context(tc.tile_pool(name="keep", bufs=1))
         outp = ctx.enter_context(tc.tile_pool(name="outp", bufs=2))
-        pst = ctx.enter_context(tc.psum_pool(name="pst", bufs=6))
-        psm = ctx.enter_context(tc.psum_pool(name="psm", bufs=2))
+        psx = ctx.enter_context(tc.psum_pool(name="psx", bufs=2))
+        ps0 = ctx.enter_context(tc.psum_pool(name="ps0", bufs=4))
+        ps1 = ctx.enter_context(tc.psum_pool(name="ps1", bufs=2))
 
         warm = const.tile([P, 8], F32, name="warm")
         nc.vector.memset(warm[:], 0.0)
         warm2 = const.tile([P, 8], F32, name="warm2")
-        nc.scalar.activation(out=warm2[:], in_=warm[:], func=AF.Sigmoid)
+        nc.scalar.activation(out=warm2[:], in_=warm[:], func=AF.Tanh)
         ident = const.tile([P, P], F32, name="ident")
         make_identity(nc, ident[:])
-        ident_bf = const.tile([P, P], BF16, name="ident_bf")
-        make_identity(nc, ident_bf[:])
         zero = const.tile([P, K_IN], F32, name="zero")
         nc.gpsimd.memset(zero[:], 0.0)
 
@@ -78,15 +80,18 @@ def tile_predictionbilstm_t_v_kernel(
         v_scales = keep.tile([P, 2, K_IN], U8, name="v_scales", align_bytes=64)
         tm_codes = keep.tile([P, 2, 3 * H], U32, name="tm_codes", align_bytes=64)
         tm_scales = keep.tile([P, 2, 3 * H], U8, name="tm_scales", align_bytes=64)
-        ff_codes = keep.tile([P, 3, 8, P], U32, name="ff_codes", align_bytes=64)
-        ff_scales = keep.tile([P, 3, 8, P], U8, name="ff_scales", align_bytes=64)
+        ft_codes = keep.tile([P, 6, 8, P], U32, name="ft_codes", align_bytes=64)
+        ft_scales = keep.tile([P, 6, 8, P], U8, name="ft_scales", align_bytes=64)
 
-        zi, zgo, dh, pt = {}, {}, {}, {}
-        gg, g2, cc, tt, t2 = {}, {}, {}, {}, {}
-        bank = {}
-        gz = {}
-        fb_codes, fb_scales = {}, {}
+        zi, zgo, dh = {}, {}, {}
+        c2, tt, t2, g2, pp = {}, {}, {}, {}, {}
+        dzt = {}
+        xts, gts = {}, {}
         raws, grps = {}, {}
+        acc0 = {}
+        o0s = {}
+        pending = []
+        flushed = [0]
 
         def sub(s):
             return s // 4, (s % 4) // 2, s % 2
@@ -100,8 +105,9 @@ def tile_predictionbilstm_t_v_kernel(
             zgo_t = zin.tile([P, 2, 2 * H], F32, name="zgo")
             if s == 0:
                 for jj in range(2):
-                    nc.sync.dma_start(out=zgo_t[:, jj, 0:H], in_=gsrc[:, jj, 2 * H : 3 * H])
                     nc.sync.dma_start(out=zi_t[:, jj, :], in_=gsrc[:, jj, 0:H])
+                    nc.sync.dma_start(out=zgo_t[:, jj, 0:H], in_=gsrc[:, jj, 2 * H : 3 * H])
+                load_w(0)
                 nc.sync.dma_start(out=zgo_t[:, :, H : 2 * H], in_=gsrc[:, js, 3 * H : 4 * H])
             else:
                 nc.sync.dma_start(out=zi_t[:], in_=gsrc[:, js, 0:H])
@@ -111,121 +117,135 @@ def tile_predictionbilstm_t_v_kernel(
             nc.sync.dma_start(out=dh_t[:], in_=dsrc[:, js, :])
             zi[s], zgo[s], dh[s] = zi_t, zgo_t, dh_t
 
+        WHOLE = (0, 2)
+
+        def parts(s):
+            return ((0, 1), (1, 2)) if s in (0, NSUB - 1) else (WHOLE,)
+
+        def a_of(s, pa):
+            return zi[s][:, pa[0] : pa[1], :]
+
+        def g_of(s, pa):
+            return zgo[s][:, pa[0] : pa[1], 0:H]
+
+        def b_of(s, pa):
+            return zgo[s][:, pa[0] : pa[1], H : 2 * H]
+
+        def cut(t_ap, pa):
+            return t_ap[:, pa[0] : pa[1], :]
+
+        def act_ag(s, pa):
+            nc.scalar.activation(out=a_of(s, pa), in_=a_of(s, pa), func=AF.Tanh, scale=0.5)
+            nc.scalar.activation(out=g_of(s, pa), in_=g_of(s, pa), func=AF.Tanh)
+
+        def act_b(s):
+            nc.scalar.activation(out=b_of(s, WHOLE), in_=b_of(s, WHOLE), func=AF.Tanh, scale=0.5)
+
         def stt(out, in0, scalar, in1, op0):
             nc.vector.scalar_tensor_tensor(out=out, in0=in0, scalar=scalar, in1=in1, op0=op0, op1=ALU.mult)
 
-        def act_io(s):
-            if s == 0:
-                for jj in range(2):
-                    nc.scalar.activation(out=zi[s][:, jj, :], in_=zi[s][:, jj, :], func=AF.Sigmoid)
-            else:
-                nc.scalar.activation(out=zi[s][:], in_=zi[s][:], func=AF.Sigmoid)
-            o_ap = zgo[s][:, :, H : 2 * H]
-            nc.scalar.activation(out=o_ap, in_=o_ap, func=AF.Sigmoid)
+        def v_c2(s, pa):
+            if pa[0] == 0:
+                c2_t = tmp.tile([P, 2, H], F32, name="c2")
+                c2[s] = c2_t
+            stt(cut(c2[s], pa), a_of(s, pa), 1.0, g_of(s, pa), ALU.add)
 
-        def gp_p(s):
-            p_t = zin.tile([P, 2, H], F32, name="pt", bufs=2)
-            pt[s] = p_t
-            nc.gpsimd.tensor_tensor(out=p_t[:], in0=zgo[s][:, :, H : 2 * H], in1=dh[s][:], op=ALU.mult)
+        def act_c(s):
+            t_t = tmp.tile([P, 2, H], F32, name="tt")
+            tt[s] = t_t
+            nc.scalar.activation(out=t_t[:], in_=c2[s][:], func=AF.Tanh, scale=0.5)
+            t2_t = tmp.tile([P, 2, H], F32, name="t2")
+            t2[s] = t2_t
+            nc.scalar.activation(out=t2_t[:], in_=t_t[:], func=AF.Square)
+            g2_t = tmp.tile([P, 2, H], F32, name="g2")
+            g2[s] = g2_t
+            nc.scalar.activation(out=g2_t[:], in_=g_of(s, WHOLE), func=AF.Square, scale=0.5)
 
-        def turn(key, src, c0):
-            b_t = pst.tile([P, 4, P], F32, name="bk")
-            bank[key] = b_t
-            for t in range(4):
-                nc.tensor.transpose(b_t[:, t, :], src[:, c0 + t : c0 + H : 4], ident[:])
-
-        def view(key):
-            return bank[key][:].rearrange("q t n -> q n t")
-
-        def new_fm(store, s, name, bufs):
-            x_t = fm.tile([P, 2, P, 4], F32, name=name, bufs=bufs)
-            store[s] = x_t
-
-        def stage_b1(s):
-            new_fm(gg, s, "gg", 2)
-            new_fm(cc, s, "cc", 3)
-            for jj in range(2):
-                turn(("z", s, jj), zgo[s][:, jj, :], 0)
-                nc.scalar.activation(out=gg[s][:, jj], in_=view(("z", s, jj)), func=AF.Tanh)
-                turn(("i", s, jj), zi[s][:, jj, :], 0)
-                nc.vector.tensor_tensor(out=cc[s][:, jj], in0=view(("i", s, jj)), in1=gg[s][:, jj], op=ALU.mult)
-            new_fm(g2, s, "g2", 3)
-            nc.scalar.activation(out=g2[s][:], in_=gg[s][:], func=AF.Square)
-            new_fm(tt, s, "tt", 2)
-            nc.scalar.activation(out=tt[s][:], in_=cc[s][:], func=AF.Tanh, scale=-1.0)
-            new_fm(t2, s, "t2", 3)
-            nc.scalar.activation(out=t2[s][:], in_=tt[s][:], func=AF.Square)
-
-        def stage_b2(s):
-            for jj in range(2):
-                stt(g2[s][:, jj], g2[s][:, jj], 1.0, view(("i", s, jj)), ALU.subtract)
-            for jj in range(2):
-                stt(cc[s][:, jj], view(("i", s, jj)), 1.0, cc[s][:, jj], ALU.subtract)
-
-        def stage_c(s, tail_on_vector):
-            gz_t = gp.tile([P, 3, 2, P, 4], BF16, name="gz", align_bytes=64)
-            gz[s] = gz_t
-            for jj in range(2):
-                turn(("o", s, jj), zgo[s][:, jj, :], H)
-                turn(("p", s, jj), pt[s][:, jj, :], 0)
-                stt(tt[s][:, jj], view(("o", s, jj)), 1.0, tt[s][:, jj], ALU.subtract)
-                stt(t2[s][:, jj], t2[s][:, jj], 1.0, view(("p", s, jj)), ALU.subtract)
-                nc.vector.tensor_tensor(out=gz_t[:, GO, jj], in0=view(("p", s, jj)), in1=tt[s][:, jj], op=ALU.mult)
-            eng = nc.vector if tail_on_vector else nc.gpsimd
-            eng.tensor_tensor(out=gz_t[:, GI], in0=t2[s][:], in1=cc[s][:], op=ALU.mult)
-            eng.tensor_tensor(out=gz_t[:, GG], in0=t2[s][:], in1=g2[s][:], op=ALU.mult)
-
-        def ft_slices(s, x):
+        def dz_out(s, x, pa):
             d, h, jp = sub(s)
-            if d == 0:
-                a0 = 4 * h + 2 * jp
-                return ff_codes[:, x, a0 : a0 + 2, :], ff_scales[:, x, a0 : a0 + 2, :]
-            return fb_codes[s][:, x], fb_scales[s][:, x]
+            return dzt[(d, h)][:, x, 2 * jp + pa[0] : 2 * jp + pa[1], :]
 
-        def quant_t(s, x):
+        def v_first(s, pa):
             d, h, jp = sub(s)
-            if d == 1 and s not in fb_codes:
-                c_t = gp.tile([P, 3, 2, P], U32, name="fbc", bufs=2, align_bytes=64)
-                s_t = gp.tile([P, 3, 2, P], U8, name="fbs", bufs=2, align_bytes=64)
-                fb_codes[s], fb_scales[s] = c_t, s_t
-            codes, scales = ft_slices(s, x)
+            if jp == 0 and pa[0] == 0:
+                dz_t = dzp.tile([P, 3, 4, H], BF16, name="dz")
+                dzt[(d, h)] = dz_t
+            if pa[0] == 0:
+                p_t = tmp.tile([P, 2, H], F32, name="pp", bufs=1)
+                pp[s] = p_t
+            stt(cut(pp[s], pa), b_of(s, pa), 1.0, cut(dh[s], pa), ALU.add)
+            stt(cut(tt[s], pa), b_of(s, pa), 1.0, cut(tt[s], pa), ALU.subtract)
+            stt(cut(t2[s], pa), cut(t2[s], pa), 1.0, cut(pp[s], pa), ALU.subtract)
+            stt(dz_out(s, GO, pa), cut(tt[s], pa), -0.25, cut(pp[s], pa), ALU.mult)
+
+        def v_second(s, pa):
+            stt(cut(c2[s], pa), a_of(s, pa), 1.0, cut(c2[s], pa), ALU.subtract)
+            stt(cut(pp[s], pa), a_of(s, pa), 1.0, cut(t2[s], pa), ALU.add)
+            stt(dz_out(s, GI, pa), cut(t2[s], pa), 0.125, cut(c2[s], pa), ALU.mult)
+
+        def v_third(s, pa):
+            stt(dz_out(s, GG, pa), cut(g2[s], pa), 0.25, cut(pp[s], pa), ALU.subtract)
+
+        def transposes(s, x, pa):
+            d, h, jp = sub(s)
+            xt = psx.tile([P, pa[1] - pa[0], 2, P], F32, name="xt")
+            xts[(s, x, pa)] = xt
+            for jj in range(pa[0], pa[1]):
+                words = dzt[(d, h)][:, x, 2 * jp + jj, :].bitcast(F32)
+                for u in range(2):
+                    nc.tensor.transpose(xt[:, jj - pa[0], u, :], words[:, u : H // 2 : 2], ident[:])
+
+        def evac_t(s, x, pa):
+            gt = stage.tile([P, pa[1] - pa[0], P, 4], BF16, name="gt", align_bytes=64)
+            gts[(s, x, pa)] = gt
+            nc.scalar.copy(out=gt[:].bitcast(F32), in_=xts[(s, x, pa)][:].rearrange("q a u p -> q a p u"))
+
+        def quant_t(s, x, pa):
+            d, h, jp = sub(s)
+            a0 = 4 * h + 2 * jp
+            g = 3 * d + x
             nc.vector.quantize_mx(
-                out=codes.rearrange("q a p -> q (a p)").bitcast(E5),
-                scales=scales.rearrange("q a p -> q (a p)"),
-                in_=gz[s][:, x].rearrange("q a p t -> q (a p t)"),
+                out=ft_codes[:, g, a0 + pa[0] : a0 + pa[1], :].rearrange("q a p -> q (a p)").bitcast(E5),
+                scales=ft_scales[:, g, a0 + pa[0] : a0 + pa[1], :].rearrange("q a p -> q (a p)"),
+                in_=gts[(s, x, pa)][:].rearrange("q a p t -> q (a p t)"),
             )
 
-        def unit0(s, jj, o0):
-            acc = psm.tile([P, K_IN], F32, name="pm")
-            for g in range(6):
-                codes, scales = ft_slices(s - 4 * (1 - g // 3), g % 3)
+        def mm0(s, g, pa, start, stop):
+            d, h, jp = sub(s)
+            for jj in range(pa[0], pa[1]):
+                a = 4 * h + 2 * jp + jj
                 nc.tensor.matmul_mx(
-                    out=acc[:],
-                    lhsT=codes[:, jj, :].bitcast(E5),
-                    lhsT_scale=scales[:, jj, :],
+                    out=acc0[(s, jj)][:],
+                    lhsT=ft_codes[:, g, a, :].bitcast(E5),
+                    lhsT_scale=ft_scales[:, g, a, :],
                     rhs=w_codes[:, g, :].bitcast(E4),
                     rhs_scale=w_scales[:, g, :],
-                    start=(g == 0),
-                    stop=(g == 5),
+                    start=start,
+                    stop=stop,
                 )
-            if jj == 0:
-                nc.scalar.copy(out=o0[:, jj, :], in_=acc[:])
-            else:
-                nc.vector.tensor_copy(out=o0[:, jj, :], in_=acc[:])
 
-        def stage_q(s):
+        def mm0_open(s):
+            for jj in range(2):
+                acc = ps0.tile([P, K_IN], F32, name="acc0")
+                acc0[(s, jj)] = acc
+            for g in range(3):
+                mm0(s, g, WHOLE, g == 0, False)
+
+        def finish0(s, pa):
             d, h, jp = sub(s)
-            for x in (GO, GI, GG):
-                quant_t(s, x)
-            if d == 1:
-                o0 = outp.tile([P, 2, K_IN], F32, name="o0")
-                for jj in range(2):
-                    unit0(s, jj, o0)
-                dst = out_0[512 * h : 512 * (h + 1), :].rearrange("(p j) c -> p j c", j=4)
-                nc.sync.dma_start(out=dst[:, 2 * jp : 2 * jp + 2, :], in_=o0[:])
+            if pa[0] == 0:
+                o0_t = outp.tile([P, 2, K_IN], F32, name="o0")
+                o0s[s] = o0_t
+            for jj in range(pa[0], pa[1]):
+                if jj == 1 and s == NSUB - 1:
+                    nc.vector.tensor_copy(out=o0s[s][:, jj, :], in_=acc0[(s, jj)][:])
+                else:
+                    nc.scalar.copy(out=o0s[s][:, jj, :], in_=acc0[(s, jj)][:])
+            dst = out_0[512 * h : 512 * (h + 1), :].rearrange("(p j) c -> p j c", j=4)
+            nc.sync.dma_start(out=dst[:, 2 * jp + pa[0] : 2 * jp + pa[1], :], in_=cut(o0s[s], pa))
 
         def load_rows(key, src):
-            raw = stage.tile([P, 4, K_IN], BF16, name="raw", bufs=3)
+            raw = stage.tile([P, 4, K_IN], BF16, name="raw")
             raws[key] = raw
             nc.sync.dma_start(out=raw[:], in_=src.rearrange("(p j) c -> p j c", j=4))
 
@@ -236,46 +256,45 @@ def tile_predictionbilstm_t_v_kernel(
         def load_v(h):
             load_rows(("v", h), V_cells[512 * h : 512 * (h + 1), :])
 
-        def prep_rows(key, codes, scales, on_vector):
+        def interleave(key, src, on_vector):
             grp = stage.tile([P, K_IN, 4], BF16, name="grp", align_bytes=64)
-            src = raws[key][:].rearrange("p j c -> p c j")
+            grps[key] = grp
+            dst4 = grp[:].rearrange("p (c i) j -> p c j i", i=4)
+            src4 = src.rearrange("p j (c i) -> p c j i", i=4)
             if on_vector:
-                nc.vector.tensor_copy(out=grp[:], in_=src)
+                nc.vector.tensor_copy(out=dst4, in_=src4)
             else:
-                nc.scalar.copy(out=grp[:], in_=src)
-            nc.vector.quantize_mx(out=codes.bitcast(E4), scales=scales, in_=grp[:].rearrange("p c j -> p (c j)"))
+                nc.scalar.copy(out=dst4, in_=src4)
+
+        def quant_rows(key, codes, scales, fmt):
+            pending.append((key, codes, scales, fmt))
+
+        def flush():
+            for key, codes, scales, fmt in pending[flushed[0] :]:
+                nc.vector.quantize_mx(
+                    out=codes.bitcast(fmt),
+                    scales=scales,
+                    in_=grps[key][:].rearrange("p c j -> p (c j)"),
+                )
+            flushed[0] = len(pending)
 
         def prep_w(g, on_vector):
-            prep_rows(("w", g), w_codes[:, g, :], w_scales[:, g, :], on_vector)
+            interleave(("w", g), raws[("w", g)][:], on_vector)
+            quant_rows(("w", g), w_codes[:, g, :], w_scales[:, g, :], E4)
 
         def prep_v(h, on_vector):
-            prep_rows(("v", h), v_codes[:, h, :], v_scales[:, h, :], on_vector)
+            interleave(("v", h), raws[("v", h)][:], on_vector)
+            quant_rows(("v", h), v_codes[:, h, :], v_scales[:, h, :], E4)
 
         def prep_tm(h, x, on_vector):
-            tmg = stage.tile([P, 4, P, 4], BF16, name="tmg", align_bytes=64)
-            for tp in range(2):
-                xt = psm.tile([P, 2, 4, P], BF16, name="pm")
-                for t in range(2):
-                    for j in range(4):
-                        src = gz[2 * h + j // 2][:, x, j % 2, :, 2 * tp + t]
-                        nc.tensor.transpose(xt[:, t, j, :], src, ident_bf[:])
-                dst = tmg[:, 2 * tp : 2 * tp + 2]
-                if on_vector[tp]:
-                    nc.vector.tensor_copy(out=dst, in_=xt[:].rearrange("p t j q -> p t q j"))
-                else:
-                    nc.scalar.copy(out=dst, in_=xt[:].rearrange("p t j q -> p t q j"))
+            interleave(("t", h, x), dzt[(0, h)][:, x, :, :], on_vector)
             cols = slice(H * x, H * (x + 1))
-            nc.vector.quantize_mx(
-                out=tm_codes[:, h, cols].bitcast(E5),
-                scales=tm_scales[:, h, cols],
-                in_=tmg[:].rearrange("p t q j -> p (t q j)"),
-            )
+            quant_rows(("t", h, x), tm_codes[:, h, cols], tm_scales[:, h, cols], E5)
 
         def out1(x):
-            rows = out_1[W_ROW0[x] : W_ROW0[x] + H, :].rearrange("(q t) c -> q t c", t=4)
-            for t in range(4):
-                cols = slice(H * x + P * t, H * x + P * (t + 1))
-                acc = psm.tile([P, K_IN], F32, name="pm")
+            for m in range(4):
+                cols = slice(H * x + P * m, H * x + P * (m + 1))
+                acc = ps1.tile([P, K_IN], F32, name="acc1")
                 for h in range(2):
                     nc.tensor.matmul_mx(
                         out=acc[:],
@@ -288,63 +307,93 @@ def tile_predictionbilstm_t_v_kernel(
                     )
                 o1 = outp.tile([P, K_IN], F32, name="o1", bufs=3)
                 nc.scalar.copy(out=o1[:], in_=acc[:])
-                nc.sync.dma_start(out=rows[:, t, :], in_=o1[:])
+                r0 = W_ROW0[x] + P * m
+                nc.sync.dma_start(out=out_1[r0 : r0 + P, :], in_=o1[:])
 
-        def extras(k):
-            if k == 0:
-                prep_w(0, True)
+        def late(s, pa):
+            d, h, jp = sub(s)
+            quant_t(s, GI, pa)
+            if d == 1:
+                mm0(s, 3 + GI, pa, False, False)
+            quant_t(s, GG, pa)
+            if d == 1:
+                mm0(s, 3 + GG, pa, False, True)
+                finish0(s, pa)
+
+        def extras(s):
+            if s == 0:
                 prep_w(1, True)
-                prep_v(0, False)
-                load_w(2)
-                load_w(3)
-                load_v(1)
-            if k == 1:
                 prep_w(2, True)
-                prep_w(3, True)
-                prep_v(1, False)
+                load_w(3)
                 load_w(4)
+                load_v(0)
+            if s == 1:
+                prep_w(3, False)
+                prep_w(4, False)
+                prep_v(0, False)
                 load_w(5)
-            if k == 2:
-                prep_w(4, True)
-                prep_w(5, True)
+                load_v(1)
+            if s == 2:
+                prep_w(5, False)
+                prep_v(1, False)
+                prep_tm(0, GO, False)
                 for r in range(4):
                     nc.sync.dma_start(out=out_1[H + P * r : H + P * (r + 1), :], in_=zero[:])
-                prep_tm(0, GO, (False, False))
-                prep_tm(0, GI, (False, True))
-                prep_tm(0, GG, (False, False))
-            if k == 4:
-                prep_tm(1, GO, (False, False))
-                prep_tm(1, GI, (False, True))
-                prep_tm(1, GG, (False, False))
-            if k == 5:
+            if s == 3:
+                prep_tm(0, GI, False)
+                prep_tm(0, GG, False)
+            if s == 4:
+                prep_tm(1, GO, True)
+                prep_tm(1, GI, True)
+                prep_tm(1, GG, False)
+            if s == 5:
                 out1(GO)
                 out1(GI)
-            if k == 6:
+            if s == 6:
                 out1(GG)
 
-        load_w(0)
         load(0)
-        load_w(1)
         load(1)
-        load_v(0)
+        load_w(1)
+        load_w(2)
         load(2)
-        act_io(0)
-        gp_p(0)
-        stage_b1(0)
-        stage_b2(0)
-        act_io(1)
-        gp_p(1)
-        for k in range(NSUB):
-            if k + 1 < NSUB:
-                stage_b1(k + 1)
-                stage_b2(k + 1)
-            stage_c(k, k == NSUB - 1)
-            if k + 3 < NSUB:
-                load(k + 3)
-            if k + 2 < NSUB:
-                act_io(k + 2)
-                gp_p(k + 2)
-            if k >= 1:
-                stage_q(k - 1)
-            extras(k)
-        stage_q(NSUB - 1)
+        load(3)
+        for pa in parts(0):
+            act_ag(0, pa)
+            v_c2(0, pa)
+        prep_w(0, True)
+        act_c(0)
+        act_b(0)
+        act_ag(1, WHOLE)
+        act_b(1)
+        for s in range(NSUB):
+            if s + 1 < NSUB:
+                v_c2(s + 1, WHOLE)
+                act_c(s + 1)
+            if s >= 1:
+                late(s - 1, WHOLE)
+            if s >= 4:
+                mm0_open(s)
+            tail = parts(s) if s == NSUB - 1 else (WHOLE,)
+            for pa in tail:
+                v_first(s, pa)
+                flush()
+                transposes(s, GO, pa)
+                if s + 2 < NSUB:
+                    act_ag(s + 2, WHOLE)
+                    act_b(s + 2)
+                evac_t(s, GO, pa)
+                v_second(s, pa)
+                transposes(s, GI, pa)
+                evac_t(s, GI, pa)
+                quant_t(s, GO, pa)
+                if s >= 4:
+                    mm0(s, 3 + GO, pa, False, False)
+                v_third(s, pa)
+                transposes(s, GG, pa)
+                evac_t(s, GG, pa)
+                if s == NSUB - 1:
+                    late(s, pa)
+            extras(s)
+            if s + 4 < NSUB:
+                load(s + 4)

@@ -62,8 +62,8 @@ def tile_predictionbilstm_t_v_kernel(
         keep = ctx.enter_context(tc.tile_pool(name="keep", bufs=1))
         outp = ctx.enter_context(tc.tile_pool(name="outp", bufs=2))
         psx = ctx.enter_context(tc.psum_pool(name="psx", bufs=2))
-        ps0 = ctx.enter_context(tc.psum_pool(name="ps0", bufs=4))
-        ps1 = ctx.enter_context(tc.psum_pool(name="ps1", bufs=2))
+        ps0 = ctx.enter_context(tc.psum_pool(name="ps0", bufs=2))
+        ps1 = ctx.enter_context(tc.psum_pool(name="ps1", bufs=4))
 
         warm = const.tile([P, 8], F32, name="warm")
         nc.vector.memset(warm[:], 0.0)
@@ -71,6 +71,8 @@ def tile_predictionbilstm_t_v_kernel(
         nc.scalar.activation(out=warm2[:], in_=warm[:], func=AF.Tanh)
         ident = const.tile([P, P], F32, name="ident")
         make_identity(nc, ident[:])
+        ident_bf = const.tile([P, P], BF16, name="ident_bf")
+        make_identity(nc, ident_bf[:])
         zero = const.tile([P, K_IN], F32, name="zero")
         nc.gpsimd.memset(zero[:], 0.0)
 
@@ -90,6 +92,7 @@ def tile_predictionbilstm_t_v_kernel(
         raws, grps = {}, {}
         acc0 = {}
         o0s = {}
+        acc1 = {}
         pending = []
         flushed = [0]
 
@@ -266,6 +269,22 @@ def tile_predictionbilstm_t_v_kernel(
             else:
                 nc.scalar.copy(out=dst4, in_=src4)
 
+        def interleave_pe(key, src):
+            grp = stage.tile([P, K_IN, 4], BF16, name="grp", align_bytes=64)
+            grps[key] = grp
+            for half in range(2):
+                pb = ps1.tile([P, 2 * P, 4], BF16, name="acc1")
+                for k in range(2):
+                    c0 = 2 * P * half + P * k
+                    nc.tensor.matmul(
+                        out=pb[:, P * k : P * (k + 1), :],
+                        lhsT=ident_bf[:],
+                        rhs=src[:, :, c0 : c0 + P].rearrange("p j c -> p c j"),
+                        start=True,
+                        stop=True,
+                    )
+                nc.scalar.copy(out=grp[:, 2 * P * half : 2 * P * (half + 1), :], in_=pb[:])
+
         def quant_rows(key, codes, scales, fmt):
             pending.append((key, codes, scales, fmt))
 
@@ -279,11 +298,14 @@ def tile_predictionbilstm_t_v_kernel(
             flushed[0] = len(pending)
 
         def prep_w(g, on_vector):
-            interleave(("w", g), raws[("w", g)][:], on_vector)
+            if on_vector is None:
+                interleave_pe(("w", g), raws[("w", g)][:])
+            else:
+                interleave(("w", g), raws[("w", g)][:], on_vector)
             quant_rows(("w", g), w_codes[:, g, :], w_scales[:, g, :], E4)
 
         def prep_v(h, on_vector):
-            interleave(("v", h), raws[("v", h)][:], on_vector)
+            interleave_pe(("v", h), raws[("v", h)][:])
             quant_rows(("v", h), v_codes[:, h, :], v_scales[:, h, :], E4)
 
         def prep_tm(h, x, on_vector):
@@ -291,10 +313,11 @@ def tile_predictionbilstm_t_v_kernel(
             cols = slice(H * x, H * (x + 1))
             quant_rows(("t", h, x), tm_codes[:, h, cols], tm_scales[:, h, cols], E5)
 
-        def out1(x):
+        def out1_mm(x):
             for m in range(4):
                 cols = slice(H * x + P * m, H * x + P * (m + 1))
                 acc = ps1.tile([P, K_IN], F32, name="acc1")
+                acc1[(x, m)] = acc
                 for h in range(2):
                     nc.tensor.matmul_mx(
                         out=acc[:],
@@ -305,8 +328,14 @@ def tile_predictionbilstm_t_v_kernel(
                         start=(h == 0),
                         stop=(h == 1),
                     )
-                o1 = outp.tile([P, K_IN], F32, name="o1", bufs=3)
-                nc.scalar.copy(out=o1[:], in_=acc[:])
+
+        def out1_store(x, on_vector):
+            for m in range(4):
+                o1 = outp.tile([P, K_IN], F32, name="o1", bufs=4)
+                if on_vector:
+                    nc.vector.tensor_copy(out=o1[:], in_=acc1[(x, m)][:])
+                else:
+                    nc.scalar.copy(out=o1[:], in_=acc1[(x, m)][:])
                 r0 = W_ROW0[x] + P * m
                 nc.sync.dma_start(out=out_1[r0 : r0 + P, :], in_=o1[:])
 
@@ -322,19 +351,19 @@ def tile_predictionbilstm_t_v_kernel(
 
         def extras(s):
             if s == 0:
-                prep_w(1, True)
-                prep_w(2, True)
+                prep_w(1, None)
+                prep_w(2, None)
                 load_w(3)
                 load_w(4)
                 load_v(0)
             if s == 1:
-                prep_w(3, False)
-                prep_w(4, False)
+                prep_w(3, None)
+                prep_w(4, None)
                 prep_v(0, False)
                 load_w(5)
                 load_v(1)
             if s == 2:
-                prep_w(5, False)
+                prep_w(5, None)
                 prep_v(1, False)
                 prep_tm(0, GO, False)
                 for r in range(4):
@@ -343,14 +372,16 @@ def tile_predictionbilstm_t_v_kernel(
                 prep_tm(0, GI, False)
                 prep_tm(0, GG, False)
             if s == 4:
-                prep_tm(1, GO, True)
-                prep_tm(1, GI, True)
+                prep_tm(1, GO, False)
+                prep_tm(1, GI, False)
                 prep_tm(1, GG, False)
             if s == 5:
-                out1(GO)
-                out1(GI)
+                out1_mm(GO)
+                out1_store(GO, False)
+                out1_mm(GI)
+                out1_store(GI, False)
             if s == 6:
-                out1(GG)
+                out1_mm(GG)
 
         load(0)
         load(1)
@@ -397,3 +428,4 @@ def tile_predictionbilstm_t_v_kernel(
             extras(s)
             if s + 4 < NSUB:
                 load(s + 4)
+        out1_store(GG, True)

@@ -71,8 +71,6 @@ def tile_predictionbilstm_t_v_kernel(
         nc.scalar.activation(out=warm2[:], in_=warm[:], func=AF.Tanh)
         ident = const.tile([P, P], F32, name="ident")
         make_identity(nc, ident[:])
-        ident_bf = const.tile([P, P], BF16, name="ident_bf")
-        make_identity(nc, ident_bf[:])
         zero = const.tile([P, K_IN], F32, name="zero")
         nc.gpsimd.memset(zero[:], 0.0)
 
@@ -269,22 +267,6 @@ def tile_predictionbilstm_t_v_kernel(
             else:
                 nc.scalar.copy(out=dst4, in_=src4)
 
-        def interleave_pe(key, src):
-            grp = stage.tile([P, K_IN, 4], BF16, name="grp", align_bytes=64)
-            grps[key] = grp
-            for half in range(2):
-                pb = ps1.tile([P, 2 * P, 4], BF16, name="acc1")
-                for k in range(2):
-                    c0 = 2 * P * half + P * k
-                    nc.tensor.matmul(
-                        out=pb[:, P * k : P * (k + 1), :],
-                        lhsT=ident_bf[:],
-                        rhs=src[:, :, c0 : c0 + P].rearrange("p j c -> p c j"),
-                        start=True,
-                        stop=True,
-                    )
-                nc.scalar.copy(out=grp[:, 2 * P * half : 2 * P * (half + 1), :], in_=pb[:])
-
         def quant_rows(key, codes, scales, fmt):
             pending.append((key, codes, scales, fmt))
 
@@ -298,14 +280,11 @@ def tile_predictionbilstm_t_v_kernel(
             flushed[0] = len(pending)
 
         def prep_w(g, on_vector):
-            if on_vector is None:
-                interleave_pe(("w", g), raws[("w", g)][:])
-            else:
-                interleave(("w", g), raws[("w", g)][:], on_vector)
+            interleave(("w", g), raws[("w", g)][:], on_vector)
             quant_rows(("w", g), w_codes[:, g, :], w_scales[:, g, :], E4)
 
         def prep_v(h, on_vector):
-            interleave_pe(("v", h), raws[("v", h)][:])
+            interleave(("v", h), raws[("v", h)][:], on_vector)
             quant_rows(("v", h), v_codes[:, h, :], v_scales[:, h, :], E4)
 
         def prep_tm(h, x, on_vector):
@@ -351,19 +330,19 @@ def tile_predictionbilstm_t_v_kernel(
 
         def extras(s):
             if s == 0:
-                prep_w(1, None)
-                prep_w(2, None)
+                prep_w(1, True)
+                prep_w(2, True)
                 load_w(3)
                 load_w(4)
                 load_v(0)
             if s == 1:
-                prep_w(3, None)
-                prep_w(4, None)
+                prep_w(3, False)
+                prep_w(4, False)
                 prep_v(0, False)
                 load_w(5)
                 load_v(1)
             if s == 2:
-                prep_w(5, None)
+                prep_w(5, False)
                 prep_v(1, False)
                 prep_tm(0, GO, False)
                 for r in range(4):
@@ -372,7 +351,7 @@ def tile_predictionbilstm_t_v_kernel(
                 prep_tm(0, GI, False)
                 prep_tm(0, GG, False)
             if s == 4:
-                prep_tm(1, GO, False)
+                prep_tm(1, GO, True)
                 prep_tm(1, GI, False)
                 prep_tm(1, GG, False)
             if s == 5:

from contextlib import ExitStack

import concourse.mybir as mybir
from concourse.masks import make_identity

N_TOK, K_IN, H = 1024, 512, 512
FLOPS = 2 * N_TOK * 6 * H * K_IN + 2 * 3 * H * N_TOK * K_IN
BYTES = (
    2 * N_TOK * 3 * H * 4
    + N_TOK * 2 * H * 2
    + N_TOK * K_IN * 2
    + 2 * 3 * H * K_IN * 2
    + N_TOK * K_IN * 4
    + 4 * H * K_IN * 4
)

F32 = mybir.dt.float32
BF16 = mybir.dt.bfloat16
U32 = mybir.dt.uint32
U8 = mybir.dt.uint8
E4 = mybir.dt.float8_e4m3fn_x4
E5 = mybir.dt.float8_e5m2_x4
AF = mybir.ActivationFunctionType
ALU = mybir.AluOpType

P = 128
GI, GG, GO = 0, 1, 2
W_ROW0 = (0, 2 * H, 3 * H)
NSUB = 8
MANUAL = False


def tile_predictionbilstm_t_v_kernel(
    tc,
    V_cells,
    w_ih_f,
    w_hh_f,
    b_ih_f,
    b_hh_f,
    w_ih_b,
    w_hh_b,
    b_ih_b,
    b_hh_b,
    gates_f,
    gates_b,
    grad_out,
    out_0,
    out_1,
):
    nc = tc.nc
    gates = (gates_f, gates_b)
    w_ih = (w_ih_f, w_ih_b)

    with ExitStack() as ctx:
        if MANUAL:
            ctx.enter_context(tc.manual_schedule())
        const = ctx.enter_context(tc.tile_pool(name="const", bufs=1))
        zin = ctx.enter_context(tc.tile_pool(name="zin", bufs=4))
        tmp = ctx.enter_context(tc.tile_pool(name="tmp", bufs=2))
        dzp = ctx.enter_context(tc.tile_pool(name="dzp", bufs=2))
        stage = ctx.enter_context(tc.tile_pool(name="stage", bufs=3))
        keep = ctx.enter_context(tc.tile_pool(name="keep", bufs=1))
        outp = ctx.enter_context(tc.tile_pool(name="outp", bufs=2))
        psx = ctx.enter_context(tc.psum_pool(name="psx", bufs=2))
        ps0 = ctx.enter_context(tc.psum_pool(name="ps0", bufs=2))
        ps1 = ctx.enter_context(tc.psum_pool(name="ps1", bufs=4))

        warm = const.tile([P, 8], F32, name="warm")
        nc.vector.memset(warm[:], 0.0)
        warm2 = const.tile([P, 8], F32, name="warm2")
        nc.scalar.activation(out=warm2[:], in_=warm[:], func=AF.Tanh)
        ident = const.tile([P, P], F32, name="ident")
        make_identity(nc, ident[:])
        zero = const.tile([P, K_IN], F32, name="zero")
        nc.gpsimd.memset(zero[:], 0.0)

        w_codes = keep.tile([P, 6, K_IN], U32, name="w_codes", align_bytes=64)
        w_scales = keep.tile([P, 6, K_IN], U8, name="w_scales", align_bytes=64)
        v_codes = keep.tile([P, 2, K_IN], U32, name="v_codes", align_bytes=64)
        v_scales = keep.tile([P, 2, K_IN], U8, name="v_scales", align_bytes=64)
        tm_codes = keep.tile([P, 2, 3 * H], U32, name="tm_codes", align_bytes=64)
        tm_scales = keep.tile([P, 2, 3 * H], U8, name="tm_scales", align_bytes=64)
        ft_codes = keep.tile([P, 6, 8, P], U32, name="ft_codes", align_bytes=64)
        ft_scales = keep.tile([P, 6, 8, P], U8, name="ft_scales", align_bytes=64)

        zi, zgo, dh = {}, {}, {}
        c2, tt, t2, g2, pp = {}, {}, {}, {}, {}
        dzt = {}
        xts, gts = {}, {}
        raws, grps = {}, {}
        acc0 = {}
        o0s = {}
        acc1 = {}
        pending = []
        flushed = [0]

        def sub(s):
            return s // 4, (s % 4) // 2, s % 2

        def load(s):
            d, h, jp = sub(s)
            rows = slice(512 * h, 512 * (h + 1))
            js = slice(2 * jp, 2 * jp + 2)
            gsrc = gates[d][rows, :].rearrange("(p j) c -> p j c", j=4)
            zi_t = zin.tile([P, 2, H], F32, name="zi")
            zgo_t = zin.tile([P, 2, 2 * H], F32, name="zgo")
            if s == 0:
                for jj in range(2):
                    nc.sync.dma_start(out=zi_t[:, jj, :], in_=gsrc[:, jj, 0:H])
                    nc.sync.dma_start(out=zgo_t[:, jj, 0:H], in_=gsrc[:, jj, 2 * H : 3 * H])
                load_w(0)
                nc.sync.dma_start(out=zgo_t[:, :, H : 2 * H], in_=gsrc[:, js, 3 * H : 4 * H])
            else:
                nc.sync.dma_start(out=zi_t[:], in_=gsrc[:, js, 0:H])
                nc.sync.dma_start(out=zgo_t[:], in_=gsrc[:, js, 2 * H : 4 * H])
            dh_t = zin.tile([P, 2, H], BF16, name="dh")
            dsrc = grad_out[rows, H * d : H * (d + 1)].rearrange("(p j) c -> p j c", j=4)
            nc.sync.dma_start(out=dh_t[:], in_=dsrc[:, js, :])
            zi[s], zgo[s], dh[s] = zi_t, zgo_t, dh_t

        WHOLE = (0, 2)

        def parts(s):
            return ((0, 1), (1, 2)) if s in (0, NSUB - 1) else (WHOLE,)

        def a_of(s, pa):
            return zi[s][:, pa[0] : pa[1], :]

        def g_of(s, pa):
            return zgo[s][:, pa[0] : pa[1], 0:H]

        def b_of(s, pa):
            return zgo[s][:, pa[0] : pa[1], H : 2 * H]

        def cut(t_ap, pa):
            return t_ap[:, pa[0] : pa[1], :]

        def act_ag(s, pa):
            nc.scalar.activation(out=a_of(s, pa), in_=a_of(s, pa), func=AF.Tanh, scale=0.5)
            nc.scalar.activation(out=g_of(s, pa), in_=g_of(s, pa), func=AF.Tanh)

        def act_b(s):
            nc.scalar.activation(out=b_of(s, WHOLE), in_=b_of(s, WHOLE), func=AF.Tanh, scale=0.5)

        def stt(out, in0, scalar, in1, op0):
            nc.vector.scalar_tensor_tensor(out=out, in0=in0, scalar=scalar, in1=in1, op0=op0, op1=ALU.mult)

        def v_c2(s, pa):
            if pa[0] == 0:
                c2_t = tmp.tile([P, 2, H], F32, name="c2")
                c2[s] = c2_t
            stt(cut(c2[s], pa), a_of(s, pa), 1.0, g_of(s, pa), ALU.add)

        def act_c(s):
            t_t = tmp.tile([P, 2, H], F32, name="tt")
            tt[s] = t_t
            nc.scalar.activation(out=t_t[:], in_=c2[s][:], func=AF.Tanh, scale=0.5)
            t2_t = tmp.tile([P, 2, H], F32, name="t2")
            t2[s] = t2_t
            nc.scalar.activation(out=t2_t[:], in_=t_t[:], func=AF.Square)
            g2_t = tmp.tile([P, 2, H], F32, name="g2")
            g2[s] = g2_t
            nc.scalar.activation(out=g2_t[:], in_=g_of(s, WHOLE), func=AF.Square, scale=0.5)

        def dz_out(s, x, pa):
            d, h, jp = sub(s)
            return dzt[(d, h)][:, x, 2 * jp + pa[0] : 2 * jp + pa[1], :]

        def v_first(s, pa):
            d, h, jp = sub(s)
            if jp == 0 and pa[0] == 0:
                dz_t = dzp.tile([P, 3, 4, H], BF16, name="dz")
                dzt[(d, h)] = dz_t
            if pa[0] == 0:
                p_t = tmp.tile([P, 2, H], F32, name="pp", bufs=1)
                pp[s] = p_t
            stt(cut(pp[s], pa), b_of(s, pa), 1.0, cut(dh[s], pa), ALU.add)
            stt(cut(tt[s], pa), b_of(s, pa), 1.0, cut(tt[s], pa), ALU.subtract)
            stt(cut(t2[s], pa), cut(t2[s], pa), 1.0, cut(pp[s], pa), ALU.subtract)
            stt(dz_out(s, GO, pa), cut(tt[s], pa), -0.25, cut(pp[s], pa), ALU.mult)

        def v_second(s, pa):
            stt(cut(c2[s], pa), a_of(s, pa), 1.0, cut(c2[s], pa), ALU.subtract)
            stt(cut(pp[s], pa), a_of(s, pa), 1.0, cut(t2[s], pa), ALU.add)
            stt(dz_out(s, GI, pa), cut(t2[s], pa), 0.125, cut(c2[s], pa), ALU.mult)

        def v_third(s, pa):
            stt(dz_out(s, GG, pa), cut(g2[s], pa), 0.25, cut(pp[s], pa), ALU.subtract)

        def transposes(s, x, pa):
            d, h, jp = sub(s)
            xt = psx.tile([P, pa[1] - pa[0], 2, P], F32, name="xt")
            xts[(s, x, pa)] = xt
            for jj in range(pa[0], pa[1]):
                words = dzt[(d, h)][:, x, 2 * jp + jj, :].bitcast(F32)
                for u in range(2):
                    nc.tensor.transpose(xt[:, jj - pa[0], u, :], words[:, u : H // 2 : 2], ident[:])

        def evac_t(s, x, pa):
            gt = stage.tile([P, pa[1] - pa[0], P, 4], BF16, name="gt", align_bytes=64)
            gts[(s, x, pa)] = gt
            nc.scalar.copy(out=gt[:].bitcast(F32), in_=xts[(s, x, pa)][:].rearrange("q a u p -> q a p u"))

        def quant_t(s, x, pa):
            d, h, jp = sub(s)
            a0 = 4 * h + 2 * jp
            g = 3 * d + x
            nc.vector.quantize_mx(
                out=ft_codes[:, g, a0 + pa[0] : a0 + pa[1], :].rearrange("q a p -> q (a p)").bitcast(E5),
                scales=ft_scales[:, g, a0 + pa[0] : a0 + pa[1], :].rearrange("q a p -> q (a p)"),
                in_=gts[(s, x, pa)][:].rearrange("q a p t -> q (a p t)"),
            )

        def mm0(s, g, pa, start, stop):
            d, h, jp = sub(s)
            for jj in range(pa[0], pa[1]):
                a = 4 * h + 2 * jp + jj
                nc.tensor.matmul_mx(
                    out=acc0[(s, jj)][:],
                    lhsT=ft_codes[:, g, a, :].bitcast(E5),
                    lhsT_scale=ft_scales[:, g, a, :],
                    rhs=w_codes[:, g, :].bitcast(E4),
                    rhs_scale=w_scales[:, g, :],
                    start=start,
                    stop=stop,
                )

        def mm0_open(s):
            for jj in range(2):
                acc = ps0.tile([P, K_IN], F32, name="acc0")
                acc0[(s, jj)] = acc
            for g in range(3):
                mm0(s, g, WHOLE, g == 0, False)

        def finish0(s, pa):
            d, h, jp = sub(s)
            if pa[0] == 0:
                o0_t = outp.tile([P, 2, K_IN], F32, name="o0")
                o0s[s] = o0_t
            for jj in range(pa[0], pa[1]):
                if jj == 1 and s == NSUB - 1:
                    nc.vector.tensor_copy(out=o0s[s][:, jj, :], in_=acc0[(s, jj)][:])
                else:
                    nc.scalar.copy(out=o0s[s][:, jj, :], in_=acc0[(s, jj)][:])
            dst = out_0[512 * h : 512 * (h + 1), :].rearrange("(p j) c -> p j c", j=4)
            nc.sync.dma_start(out=dst[:, 2 * jp + pa[0] : 2 * jp + pa[1], :], in_=cut(o0s[s], pa))

        def load_rows(key, src):
            raw = stage.tile([P, 4, K_IN], BF16, name="raw")
            raws[key] = raw
            nc.sync.dma_start(out=raw[:], in_=src.rearrange("(p j) c -> p j c", j=4))

        def load_w(g):
            d, x = g // 3, g % 3
            load_rows(("w", g), w_ih[d][W_ROW0[x] : W_ROW0[x] + H, :])

        def load_v(h):
            load_rows(("v", h), V_cells[512 * h : 512 * (h + 1), :])

        def interleave(key, src, on_vector):
            grp = stage.tile([P, K_IN, 4], BF16, name="grp", align_bytes=64)
            grps[key] = grp
            dst4 = grp[:].rearrange("p (c i) j -> p c j i", i=4)
            src4 = src.rearrange("p j (c i) -> p c j i", i=4)
            if on_vector:
                nc.vector.tensor_copy(out=dst4, in_=src4)
            else:
                nc.scalar.copy(out=dst4, in_=src4)

        def quant_rows(key, codes, scales, fmt):
            pending.append((key, codes, scales, fmt))

        def flush():
            for key, codes, scales, fmt in pending[flushed[0] :]:
                nc.vector.quantize_mx(
                    out=codes.bitcast(fmt),
                    scales=scales,
                    in_=grps[key][:].rearrange("p c j -> p (c j)"),
                )
            flushed[0] = len(pending)

        def prep_w(g, on_vector):
            interleave(("w", g), raws[("w", g)][:], on_vector)
            quant_rows(("w", g), w_codes[:, g, :], w_scales[:, g, :], E4)

        def prep_v(h, on_vector):
            interleave(("v", h), raws[("v", h)][:], on_vector)
            quant_rows(("v", h), v_codes[:, h, :], v_scales[:, h, :], E4)

        def prep_tm(h, x, on_vector):
            interleave(("t", h, x), dzt[(0, h)][:, x, :, :], on_vector)
            cols = slice(H * x, H * (x + 1))
            quant_rows(("t", h, x), tm_codes[:, h, cols], tm_scales[:, h, cols], E5)

        def out1_mm(x):
            for m in range(4):
                cols = slice(H * x + P * m, H * x + P * (m + 1))
                acc = ps1.tile([P, K_IN], F32, name="acc1")
                acc1[(x, m)] = acc
                for h in range(2):
                    nc.tensor.matmul_mx(
                        out=acc[:],
                        lhsT=tm_codes[:, h, cols].bitcast(E5),
                        lhsT_scale=tm_scales[:, h, cols],
                        rhs=v_codes[:, h, :].bitcast(E4),
                        rhs_scale=v_scales[:, h, :],
                        start=(h == 0),
                        stop=(h == 1),
                    )

        def out1_store(x, on_vector):
            for m in range(4):
                o1 = outp.tile([P, K_IN], F32, name="o1", bufs=4)
                if on_vector:
                    nc.vector.tensor_copy(out=o1[:], in_=acc1[(x, m)][:])
                else:
                    nc.scalar.copy(out=o1[:], in_=acc1[(x, m)][:])
                r0 = W_ROW0[x] + P * m
                nc.sync.dma_start(out=out_1[r0 : r0 + P, :], in_=o1[:])

        def late(s, pa):
            d, h, jp = sub(s)
            quant_t(s, GI, pa)
            if d == 1:
                mm0(s, 3 + GI, pa, False, False)
            quant_t(s, GG, pa)
            if d == 1:
                mm0(s, 3 + GG, pa, False, True)
                finish0(s, pa)

        def extras(s):
            if s == 0:
                prep_w(1, True)
                prep_w(2, True)
                load_w(3)
                load_w(4)
                load_v(0)
            if s == 1:
                prep_w(3, False)
                prep_w(4, False)
                prep_v(0, False)
                load_w(5)
                load_v(1)
            if s == 2:
                prep_w(5, False)
                prep_v(1, False)
                prep_tm(0, GO, False)
                for r in range(4):
                    nc.sync.dma_start(out=out_1[H + P * r : H + P * (r + 1), :], in_=zero[:])
            if s == 3:
                prep_tm(0, GI, False)
                prep_tm(0, GG, False)
            if s == 4:
                prep_tm(1, GO, True)
                prep_tm(1, GI, False)
                prep_tm(1, GG, False)
            if s == 5:
                out1_mm(GO)
                out1_store(GO, False)
                out1_mm(GI)
                out1_store(GI, False)
            if s == 6:
                out1_mm(GG)

        load(0)
        load(1)
        load_w(1)
        load_w(2)
        load(2)
        load(3)
        for pa in parts(0):
            act_ag(0, pa)
            v_c2(0, pa)
        prep_w(0, True)
        act_c(0)
        act_b(0)
        act_ag(1, WHOLE)
        act_b(1)
        for s in range(NSUB):
            if s + 1 < NSUB:
                v_c2(s + 1, WHOLE)
                act_c(s + 1)
            if s >= 1:
                late(s - 1, WHOLE)
            if s >= 4:
                mm0_open(s)
            tail = parts(s) if s == NSUB - 1 else (WHOLE,)
            for pa in tail:
                v_first(s, pa)
                flush()
                transposes(s, GO, pa)
                if s + 2 < NSUB:
                    act_ag(s + 2, WHOLE)
                    act_b(s + 2)
                evac_t(s, GO, pa)
                v_second(s, pa)
                transposes(s, GI, pa)
                evac_t(s, GI, pa)
                quant_t(s, GO, pa)
                if s >= 4:
                    mm0(s, 3 + GO, pa, False, False)
                v_third(s, pa)
                transposes(s, GG, pa)
                evac_t(s, GG, pa)
                if s == NSUB - 1:
                    late(s, pa)
            extras(s)
            if s + 4 < NSUB:
                load(s + 4)
        out1_store(GG, True)
